import numpy as np
import ml_dtypes


def mxq(x, axis, fmt="e4m3"):
    dtype, down = {"e4m3": (ml_dtypes.float8_e4m3fn, 7), "e5m2": (ml_dtypes.float8_e5m2, 14)}[fmt]
    v = np.moveaxis(np.asarray(x, np.float32).astype(ml_dtypes.bfloat16).astype(np.float64), axis, -1)
    blocks = v.reshape(v.shape[:-1] + (-1, 32))
    amax = np.abs(blocks).max(-1, keepdims=True)
    byte = np.maximum(np.where(amax > 0, np.frexp(amax)[1] - 1 + 127, 0) - down, 1)
    scale = np.exp2(byte - 127.0)
    codes = (blocks / scale).astype(np.float32).astype(dtype).astype(np.float64)
    return np.moveaxis((codes * scale).reshape(v.shape), -1, axis)


WIDE = False


def mx_kscale(k):
    if not WIDE:
        return np.ones(k)
    levels = np.array([10, -10, 5, -5, 0])
    a = np.random.permutation(np.resize(levels, k // 512 * 4)).reshape(k // 512, 4)
    idx = np.arange(k)
    return np.exp2(a[idx // 512, idx % 128 // 32])


BF16 = ml_dtypes.bfloat16


def bf(x):
    return np.asarray(x, np.float32).astype(BF16)


def f64(x):
    return np.asarray(x).astype(np.float64)


B, N, C = 16, 16, 1024
NEG_SLOPE = 0.2


def leaky(v):
    return np.where(v >= 0, v, NEG_SLOPE * v)


def setup_inputs():
    s, t = mx_kscale(C), mx_kscale(C)
    w1 = np.random.standard_normal((2, C, C)) * 0.7 / np.sqrt(C) / s[None, :, None] * t
    return {"F": bf(np.random.standard_normal((B, N, C)) * s),
            "W1": bf(w1.reshape(2 * C, C)),
            "b1": bf(np.random.standard_normal(C) * 0.2 * t),
            "W2": bf(np.random.standard_normal((C, C)) / np.sqrt(C) / t[:, None]),
            "b2": bf(np.random.standard_normal(C) * 0.2)}


def reference(F, W1, b1, W2, b2):
    Fq = mxq(f64(F), 2, "e4m3")
    W1 = f64(W1)
    A = Fq @ mxq(W1[:C], 0, "e4m3")
    Bp = Fq @ mxq(W1[C:], 0, "e4m3")
    h = leaky(A[:, :, None, :] + Bp[:, None, :, :] + f64(b1))
    h = leaky((mxq(h, 3, "e4m3") @ mxq(f64(W2), 0, "e4m3")) + f64(b2))
    return h.sum(-2)

@@ -1,0 +1,347 @@
+from contextlib import ExitStack
+
+import concourse.bass as bass
+import concourse.mybir as mybir
+import concourse.tile as tile
+from concourse.masks import make_identity
+
+F32 = mybir.dt.float32
+BF16 = mybir.dt.bfloat16
+U32 = mybir.dt.uint32
+U8 = mybir.dt.uint8
+FP8X4 = mybir.dt.float8_e4m3fn_x4
+ALU = mybir.AluOpType
+ACT = mybir.ActivationFunctionType
+
+P = 128
+C = 1024
+ROWS = 256
+NODES = 16
+SETS = 16
+UNITS = 8
+SLOPE = 0.2
+FLOPS = 2 * ROWS * C * 2 * C + 2 * ROWS * NODES * C * C
+
+
+def tile_nonlocalmp_pa_kernel(tc, F, W1, b1, W2, b2, out):
+    nc = tc.nc
+    f_flat = F.flatten_outer_dims()
+    out_flat = out.flatten_outer_dims()
+
+    with ExitStack() as ctx:
+        const = ctx.enter_context(tc.tile_pool(name="const", bufs=1))
+        rawp = ctx.enter_context(tc.tile_pool(name="rawp", bufs=8))
+        grpp = ctx.enter_context(tc.tile_pool(name="grpp", bufs=4))
+        up = ctx.enter_context(tc.tile_pool(name="up", bufs=2))
+        hbp = ctx.enter_context(tc.tile_pool(name="hbp", bufs=2))
+        hcp = ctx.enter_context(tc.tile_pool(name="hcp", bufs=4))
+        resp = ctx.enter_context(tc.tile_pool(name="resp", bufs=4))
+        work = ctx.enter_context(tc.psum_pool(name="work", bufs=4))
+        sigp = ctx.enter_context(tc.psum_pool(name="sigp", bufs=1))
+        ctx.enter_context(tc.manual_schedule())
+
+        ident32 = const.tile([P, P], F32, name="ident32")
+        make_identity(nc, ident32[:])
+        identb = const.tile([P, P], BF16, name="identb")
+        make_identity(nc, identb[:])
+        bt = const.tile([P, P], BF16, name="bt")
+        nc.vector.memset(bt[:], 0.0)
+
+        fsb = const.tile([P, 2, C], BF16, name="fsb")
+        fg = const.tile([P, 2, ROWS, 4], BF16, name="fg", align_bytes=64)
+        fc = const.tile([P, 2, ROWS], U32, name="fc", align_bytes=64)
+        fs = const.tile([P, 2, ROWS], U8, name="fs", align_bytes=64)
+        w1c = const.tile([P, 2, 2, 2, 512], U32, name="w1c", align_bytes=64)
+        w1s = const.tile([P, 2, 2, 2, 512], U8, name="w1s", align_bytes=64)
+        w2c = const.tile([P, 2, C], U32, name="w2c", align_bytes=64)
+        w2s = const.tile([P, 2, C], U8, name="w2s", align_bytes=64)
+        a4 = const.tile([P, 2, ROWS, 4], F32, name="a4")
+        b4 = const.tile([P, 2, ROWS, 4], F32, name="b4")
+        b1c = const.tile([P, 8], F32, name="b1c")
+        nb2 = const.tile([P, 8], F32, name="nb2")
+        b2x = const.tile([P, 8], F32, name="b2x")
+        acc = const.tile([P, 8, 512], F32, name="acc")
+        accs = const.tile([P, 8, ROWS], F32, name="accs")
+        sigsb = const.tile([P, 4, 512], F32, name="sigsb")
+
+        nc.sync.dma_start(out=fsb[:], in_=f_flat.rearrange("(f p) c -> p f c", p=P))
+        nc.sync.dma_start(out=bt[0:8, :], in_=b1.rearrange("(r c) -> r c", c=P))
+        nc.sync.dma_start(out=bt[8:16, :], in_=b2.rearrange("(r c) -> r c", c=P))
+        w1raw = {}
+        for g in range(2):
+            for ab in range(2):
+                for kp in range(2):
+                    raw = rawp.tile([P, 4, 512], BF16, name="raw")
+                    r0 = ab * C + kp * 512
+                    nc.sync.dma_start(
+                        out=raw[:],
+                        in_=W1[r0 : r0 + 512, g * 512 : (g + 1) * 512].rearrange("(p j) w -> p j w", j=4),
+                    )
+                    w1raw[(g, ab, kp)] = raw
+        w2raw = {}
+        for g in range(2):
+            for ch in range(2):
+                raw = rawp.tile([P, 4, 512], BF16, name="raw")
+                nc.sync.dma_start(
+                    out=raw[:],
+                    in_=W2[g * 512 : (g + 1) * 512, ch * 512 : (ch + 1) * 512].rearrange("(t p) n -> p t n", p=P),
+                )
+                w2raw[(g, ch)] = raw
+
+        def regroup(eng_is_vector, raw):
+            gq = grpp.tile([P, 512, 4], BF16, name="gq", align_bytes=64)
+            dst = gq[:].rearrange("p (c i) t -> p c t i", i=4)
+            src = raw[:].rearrange("p t (c i) -> p c t i", i=4)
+            if eng_is_vector:
+                nc.vector.tensor_copy(out=dst, in_=src)
+            else:
+                nc.scalar.copy(out=dst, in_=src)
+            return gq
+
+        def quant(gq, codes, scales):
+            nc.vector.quantize_mx(
+                out=codes.bitcast(FP8X4), scales=scales, in_=gq[:].rearrange("p w t -> p (w t)")
+            )
+
+        fsb32 = fsb[:].bitcast(F32)
+        fg32 = fg[:].bitcast(F32)
+        for kp in range(2):
+            xt = work.tile([P, 2, ROWS], F32, name="wk")
+            for f in range(2):
+                for u in range(2):
+                    nc.tensor.transpose(
+                        xt[:, u, f * P : (f + 1) * P],
+                        fsb32[:, f, kp * 256 + u : (kp + 1) * 256 : 2],
+                        ident32[:],
+                    )
+            nc.vector.tensor_copy(out=fg32[:, kp], in_=xt[:].rearrange("p u c -> p c u"))
+        nc.vector.quantize_mx(
+            out=fc[:].rearrange("p k c -> p (k c)").bitcast(FP8X4),
+            scales=fs[:].rearrange("p k c -> p (k c)"),
+            in_=fg[:].rearrange("p k c t -> p (k c t)"),
+        )
+        btp = work.tile([P, P], BF16, name="wk")
+        nc.tensor.transpose(btp[:], bt[:], identb[:])
+        nc.vector.tensor_copy(out=b1c[:], in_=btp[:, 0:8])
+        nc.vector.tensor_scalar_mul(out=nb2[:], in0=btp[:, 8:16], scalar1=-1.0)
+        nc.vector.tensor_scalar_mul(out=b2x[:], in0=btp[:, 8:16], scalar1=float(NODES) / (1.0 - SLOPE))
+
+        def stage1_pe(g):
+            tiles = {}
+            for ab in range(2):
+                for f in range(2):
+                    ps = work.tile([P, 4, P], F32, name="wk")
+                    for t in range(4):
+                        for kp in range(2):
+                            nc.tensor.matmul_mx(
+                                out=ps[:, t, :],
+                                lhsT=w1c[:, g, ab, kp, t * P : (t + 1) * P].bitcast(FP8X4),
+                                lhsT_scale=w1s[:, g, ab, kp, t * P : (t + 1) * P],
+                                rhs=fc[:, kp, f * P : (f + 1) * P].bitcast(FP8X4),
+                                rhs_scale=fs[:, kp, f * P : (f + 1) * P],
+                                start=(kp == 0),
+                                stop=(kp == 1),
+                            )
+                    tiles[(ab, f)] = ps
+            return tiles
+
+        def evac_a(g, tiles):
+            for f in range(2):
+                nc.vector.tensor_tensor(
+                    out=a4[:, g, f * P : (f + 1) * P, :],
+                    in0=tiles[(0, f)][:].rearrange("p t r -> p r t"),
+                    in1=b1c[:, 4 * g : 4 * g + 4].unsqueeze(1).to_broadcast([P, P, 4]),
+                    op=ALU.add,
+                )
+
+        def evac_b(g, tiles):
+            for f in range(2):
+                nc.scalar.copy(
+                    out=b4[:, g, f * P : (f + 1) * P, :],
+                    in_=tiles[(1, f)][:].rearrange("p t r -> p r t"),
+                )
+
+        g0 = {}
+        g0[0] = regroup(True, w1raw[(0, 0, 0)])
+        g0[1] = regroup(False, w1raw[(0, 0, 1)])
+        quant(g0[0], w1c[:, 0, 0, 0, :], w1s[:, 0, 0, 0, :])
+        g0[2] = regroup(True, w1raw[(0, 1, 0)])
+        g0[3] = regroup(False, w1raw[(0, 1, 1)])
+        quant(g0[1], w1c[:, 0, 0, 1, :], w1s[:, 0, 0, 1, :])
+        quant(g0[2], w1c[:, 0, 1, 0, :], w1s[:, 0, 1, 0, :])
+        quant(g0[3], w1c[:, 0, 1, 1, :], w1s[:, 0, 1, 1, :])
+        st = stage1_pe(0)
+        evac_a(0, st)
+        evac_b(0, st)
+
+        g1 = {}
+        for idx in range(4):
+            g1[idx] = regroup(False, w1raw[(1, idx // 2, idx % 2)])
+
+        sig = {}
+        for hb in range(2):
+            for ch in range(2):
+                sig[(hb, ch)] = sigp.tile([P, 512], F32, name="sig%d%d" % (hb, ch))
+        state = {"pending": None}
+        utile = {}
+        hbt = {}
+        hct = {}
+        hst = {}
+        ytile = {}
+        done_g = {}
+
+        def sigma_passes(n, hb):
+            for ch in range(2):
+                for jj in range(2):
+                    for g in range(2):
+                        c0 = jj * 256 + hb * P
+                        nc.tensor.matmul_mx(
+                            out=sig[(hb, ch)][:],
+                            lhsT=hct[n][:, g, c0 : c0 + P].bitcast(FP8X4),
+                            lhsT_scale=hst[n][:, g, c0 : c0 + P],
+                            rhs=w2c[:, g, ch * 512 : (ch + 1) * 512].bitcast(FP8X4),
+                            rhs_scale=w2s[:, g, ch * 512 : (ch + 1) * 512],
+                            start=(n == 0 and jj == 0 and g == 0),
+                            stop=(n == UNITS - 1 and jj == 1 and g == 1),
+                        )
+
+        def main_passes(n, ms):
+            for m in ms:
+                y = work.tile([P, 512], F32, name="wk")
+                for g in range(2):
+                    nc.tensor.matmul_mx(
+                        out=y[:],
+                        lhsT=w2c[:, g, m * P : (m + 1) * P].bitcast(FP8X4),
+                        lhsT_scale=w2s[:, g, m * P : (m + 1) * P],
+                        rhs=hct[n][:, g, :].bitcast(FP8X4),
+                        rhs_scale=hst[n][:, g, :],
+                        start=(g == 0),
+                        stop=(g == 1),
+                    )
+                ytile[(n, m)] = y
+
+        def pe_block(n):
+            main_passes(n, range(0, 4))
+            sigma_passes(n, 0)
+            main_passes(n, range(4, 8))
+            sigma_passes(n, 1)
+
+        def flush():
+            k = state["pending"]
+            if k is None:
+                return
+            state["pending"] = None
+            n, g = k
+            nc.vector.quantize_mx(
+                out=hct[n][:, g, :].bitcast(FP8X4), scales=hst[n][:, g, :], in_=hbt[k][:]
+            )
+            done_g[n] = done_g.get(n, 0) + 1
+            if done_g[n] == 2:
+                pe_block(n)
+
+        def h_tile(n, g):
+            if n not in hct:
+                hct[n] = hcp.tile([P, 2, 512], U32, name="hc", align_bytes=64)
+                hst[n] = hcp.tile([P, 2, 512], U8, name="hs", align_bytes=64)
+            u = up.tile([P, 2, SETS, NODES, 4], F32, name="u")
+            a_view = a4[:, g].rearrange("p (b i) t -> p b i t", i=NODES)
+            b_view = b4[:, g].rearrange("p (b j) t -> p b j t", j=NODES)
+            for jj in range(2):
+                j = 2 * n + jj
+                nc.vector.tensor_tensor(
+                    out=u[:, jj],
+                    in0=a_view,
+                    in1=b_view[:, :, j, :].unsqueeze(2).to_broadcast([P, SETS, NODES, 4]),
+                    op=ALU.add,
+                )
+                flush()
+            hb16 = hbp.tile([P, 2048], BF16, name="hb16", align_bytes=64)
+            uf = u[:].rearrange("p a b i t -> p (a b i t)")
+            nc.vector.scalar_tensor_tensor(
+                out=hb16[:], in0=uf, scalar=SLOPE, in1=uf, op0=ALU.mult, op1=ALU.max
+            )
+            hbt[(n, g)] = hb16
+            state["pending"] = (n, g)
+
+        def o_part(n, half):
+            for m in range(4 * half, 4 * half + 4):
+                y = ytile[(n, m)]
+                if n == 0:
+                    nc.vector.tensor_scalar_max(out=acc[:, m, :], in0=y[:], scalar1=nb2[:, m : m + 1])
+                else:
+                    nc.vector.scalar_tensor_tensor(
+                        out=acc[:, m, :],
+                        in0=y[:],
+                        scalar=nb2[:, m : m + 1],
+                        in1=acc[:, m, :],
+                        op0=ALU.max,
+                        op1=ALU.add,
+                    )
+                flush()
+
+        def q1(idx):
+            quant(g1[idx], w1c[:, 1, idx // 2, idx % 2, :], w1s[:, 1, idx // 2, idx % 2, :])
+            flush()
+
+        h_tile(0, 0)
+        q1(0)
+        q1(1)
+        h_tile(1, 0)
+        q1(2)
+        q1(3)
+        st = stage1_pe(1)
+        evac_b(1, st)
+        g2 = {}
+        for idx in range(4):
+            g2[idx] = regroup(False, w2raw[(idx // 2, idx % 2)])
+        h_tile(2, 0)
+        evac_a(1, st)
+        flush()
+        h_tile(0, 1)
+        for idx in range(4):
+            gg, ch = idx // 2, idx % 2
+            quant(g2[idx], w2c[:, gg, ch * 512 : (ch + 1) * 512], w2s[:, gg, ch * 512 : (ch + 1) * 512])
+        h_tile(1, 1)
+        o_part(0, 0)
+        h_tile(2, 1)
+        o_part(0, 1)
+        for n in range(3, UNITS):
+            h_tile(n, 0)
+            o_part(n - 2, 0)
+            h_tile(n, 1)
+            o_part(n - 2, 1)
+        for n in range(UNITS - 2, UNITS):
+            o_part(n, 0)
+            o_part(n, 1)
+
+        for hb in range(2):
+            for ch in range(2):
+                nc.scalar.mul(out=sigsb[:, 2 * hb + ch, :], in_=sig[(hb, ch)][:], mul=SLOPE)
+        for m in range(8):
+            nc.vector.scalar_tensor_tensor(
+                out=accs[:, m, :],
+                in0=acc[:, m, 0:256],
+                scalar=b2x[:, m : m + 1],
+                in1=acc[:, m, 256:512],
+                op0=ALU.add,
+                op1=ALU.add,
+            )
+        for ch in range(2):
+            for hb in range(2):
+                tp = work.tile([P, 4, P], F32, name="wk")
+                for mm in range(4):
+                    nc.tensor.transpose(
+                        tp[:, mm, :], accs[:, 4 * ch + mm, hb * P : (hb + 1) * P], ident32[:]
+                    )
+                res = resp.tile([P, 512], F32, name="res")
+                nc.vector.scalar_tensor_tensor(
+                    out=res[:],
+                    in0=tp[:].rearrange("p m r -> p (m r)"),
+                    scalar=1.0 - SLOPE,
+                    in1=sigsb[:, 2 * hb + ch, :],
+                    op0=ALU.mult,
+                    op1=ALU.add,
+                )
+                nc.sync.dma_start(
+                    out=out_flat[hb * P : (hb + 1) * P, ch * 512 : (ch + 1) * 512], in_=res[:]
+                )

@@ -23,6 +23,15 @@ SLOPE = 0.2
 FLOPS = 2 * ROWS * C * 2 * C + 2 * ROWS * NODES * C * C
 
 
+SEQ = [
+    (0, 0, "V", "V"), (1, 0, "V", "V"), (2, 0, "V", "V"), (3, 0, "V", "V"),
+    (4, 0, "V", "S"), (0, 1, "V", "S"), (5, 0, "V", "S"), (1, 1, "V", "S"),
+    (6, 0, "V", "S"), (2, 1, "G", "S"), (7, 0, "V", "S"), (3, 1, "G", "S"),
+    (4, 1, "V", "S"), (5, 1, "G", "S"), (6, 1, "G", "S"), (7, 1, "G", "S"),
+]
+OCAP = [0, 0, 0, 0, 0, 0, 4, 4, 4, 4, 4, 4, 8, 8, 8, 8, 8, 8]
+
+
 def tile_nonlocalmp_pa_kernel(tc, F, W1, b1, W2, b2, out):
     nc = tc.nc
     f_flat = F.flatten_outer_dims()
@@ -32,9 +41,9 @@ def tile_nonlocalmp_pa_kernel(tc, F, W1, b1, W2, b2, out):
         const = ctx.enter_context(tc.tile_pool(name="const", bufs=1))
         rawp = ctx.enter_context(tc.tile_pool(name="rawp", bufs=8))
         grpp = ctx.enter_context(tc.tile_pool(name="grpp", bufs=4))
-        up = ctx.enter_context(tc.tile_pool(name="up", bufs=2))
-        hbp = ctx.enter_context(tc.tile_pool(name="hbp", bufs=2))
-        hcp = ctx.enter_context(tc.tile_pool(name="hcp", bufs=4))
+        up = ctx.enter_context(tc.tile_pool(name="up", bufs=5))
+        hbp = ctx.enter_context(tc.tile_pool(name="hbp", bufs=3))
+        nnp = ctx.enter_context(tc.tile_pool(name="nnp", bufs=2))
         resp = ctx.enter_context(tc.tile_pool(name="resp", bufs=4))
         work = ctx.enter_context(tc.psum_pool(name="work", bufs=4))
         sigp = ctx.enter_context(tc.psum_pool(name="sigp", bufs=1))
@@ -55,20 +64,20 @@ def tile_nonlocalmp_pa_kernel(tc, F, W1, b1, W2, b2, out):
         w1s = const.tile([P, 2, 2, 2, 512], U8, name="w1s", align_bytes=64)
         w2c = const.tile([P, 2, C], U32, name="w2c", align_bytes=64)
         w2s = const.tile([P, 2, C], U8, name="w2s", align_bytes=64)
+        hc = const.tile([P, UNITS, 2, 512], U32, name="hc", align_bytes=64)
+        hs = const.tile([P, UNITS, 2, 512], U8, name="hs", align_bytes=64)
         a4 = const.tile([P, 2, ROWS, 4], F32, name="a4")
         b4 = const.tile([P, 2, ROWS, 4], F32, name="b4")
         b1c = const.tile([P, 8], F32, name="b1c")
         nb2 = const.tile([P, 8], F32, name="nb2")
         b2x = const.tile([P, 8], F32, name="b2x")
         acc = const.tile([P, 8, 512], F32, name="acc")
-        accs = const.tile([P, 8, ROWS], F32, name="accs")
-        sigsb = const.tile([P, 4, 512], F32, name="sigsb")
 
         nc.sync.dma_start(out=fsb[:], in_=f_flat.rearrange("(f p) c -> p f c", p=P))
-        nc.sync.dma_start(out=bt[0:8, :], in_=b1.rearrange("(r c) -> r c", c=P))
-        nc.sync.dma_start(out=bt[8:16, :], in_=b2.rearrange("(r c) -> r c", c=P))
         w1raw = {}
-        for g in range(2):
+        w2raw = {}
+
+        def load_w1(g):
             for ab in range(2):
                 for kp in range(2):
                     raw = rawp.tile([P, 4, 512], BF16, name="raw")
@@ -78,7 +87,11 @@ def tile_nonlocalmp_pa_kernel(tc, F, W1, b1, W2, b2, out):
                         in_=W1[r0 : r0 + 512, g * 512 : (g + 1) * 512].rearrange("(p j) w -> p j w", j=4),
                     )
                     w1raw[(g, ab, kp)] = raw
-        w2raw = {}
+
+        load_w1(0)
+        nc.sync.dma_start(out=bt[0:8, :], in_=b1.rearrange("(r c) -> r c", c=P))
+        nc.sync.dma_start(out=bt[8:16, :], in_=b2.rearrange("(r c) -> r c", c=P))
+        load_w1(1)
         for g in range(2):
             for ch in range(2):
                 raw = rawp.tile([P, 4, 512], BF16, name="raw")
@@ -120,11 +133,6 @@ def tile_nonlocalmp_pa_kernel(tc, F, W1, b1, W2, b2, out):
             scales=fs[:].rearrange("p k c -> p (k c)"),
             in_=fg[:].rearrange("p k c t -> p (k c t)"),
         )
-        btp = work.tile([P, P], BF16, name="wk")
-        nc.tensor.transpose(btp[:], bt[:], identb[:])
-        nc.vector.tensor_copy(out=b1c[:], in_=btp[:, 0:8])
-        nc.vector.tensor_scalar_mul(out=nb2[:], in0=btp[:, 8:16], scalar1=-1.0)
-        nc.vector.tensor_scalar_mul(out=b2x[:], in0=btp[:, 8:16], scalar1=float(NODES) / (1.0 - SLOPE))
 
         def stage1_pe(g):
             tiles = {}
@@ -161,15 +169,18 @@ def tile_nonlocalmp_pa_kernel(tc, F, W1, b1, W2, b2, out):
                     in_=tiles[(1, f)][:].rearrange("p t r -> p r t"),
                 )
 
-        g0 = {}
-        g0[0] = regroup(True, w1raw[(0, 0, 0)])
-        g0[1] = regroup(False, w1raw[(0, 0, 1)])
-        quant(g0[0], w1c[:, 0, 0, 0, :], w1s[:, 0, 0, 0, :])
-        g0[2] = regroup(True, w1raw[(0, 1, 0)])
-        g0[3] = regroup(False, w1raw[(0, 1, 1)])
-        quant(g0[1], w1c[:, 0, 0, 1, :], w1s[:, 0, 0, 1, :])
-        quant(g0[2], w1c[:, 0, 1, 0, :], w1s[:, 0, 1, 0, :])
-        quant(g0[3], w1c[:, 0, 1, 1, :], w1s[:, 0, 1, 1, :])
+        prev = None
+        for idx in range(4):
+            gq = regroup(True, w1raw[(0, idx // 2, idx % 2)])
+            if prev is not None:
+                quant(prev[0], w1c[:, 0, prev[1] // 2, prev[1] % 2, :], w1s[:, 0, prev[1] // 2, prev[1] % 2, :])
+            prev = (gq, idx)
+        btp = work.tile([P, P], BF16, name="wk")
+        nc.tensor.transpose(btp[:], bt[:], identb[:])
+        nc.vector.tensor_copy(out=b1c[:], in_=btp[:, 0:8])
+        quant(prev[0], w1c[:, 0, 1, 1, :], w1s[:, 0, 1, 1, :])
+        nc.vector.tensor_scalar_mul(out=nb2[:], in0=btp[:, 8:16], scalar1=-1.0)
+        nc.vector.tensor_scalar_mul(out=b2x[:], in0=btp[:, 8:16], scalar1=float(NODES) / (1.0 - SLOPE))
         st = stage1_pe(0)
         evac_a(0, st)
         evac_b(0, st)
@@ -177,33 +188,35 @@ def tile_nonlocalmp_pa_kernel(tc, F, W1, b1, W2, b2, out):
         g1 = {}
         for idx in range(4):
             g1[idx] = regroup(False, w1raw[(1, idx // 2, idx % 2)])
+        g2 = {}
 
         sig = {}
         for hb in range(2):
             for ch in range(2):
                 sig[(hb, ch)] = sigp.tile([P, 512], F32, name="sig%d%d" % (hb, ch))
-        state = {"pending": None}
+        state = {"pending": None, "w2": [False, False], "evac1": False, "sig_wait": [], "oq": []}
+        sig_count = {}
         utile = {}
         hbt = {}
-        hct = {}
-        hst = {}
+        nnt = {}
         ytile = {}
         done_g = {}
 
-        def sigma_passes(n, hb):
+        def sigma_passes(n, g, hb):
             for ch in range(2):
                 for jj in range(2):
-                    for g in range(2):
-                        c0 = jj * 256 + hb * P
-                        nc.tensor.matmul_mx(
-                            out=sig[(hb, ch)][:],
-                            lhsT=hct[n][:, g, c0 : c0 + P].bitcast(FP8X4),
-                            lhsT_scale=hst[n][:, g, c0 : c0 + P],
-                            rhs=w2c[:, g, ch * 512 : (ch + 1) * 512].bitcast(FP8X4),
-                            rhs_scale=w2s[:, g, ch * 512 : (ch + 1) * 512],
-                            start=(n == 0 and jj == 0 and g == 0),
-                            stop=(n == UNITS - 1 and jj == 1 and g == 1),
-                        )
+                    c0 = jj * 256 + hb * P
+                    cnt = sig_count.get((hb, ch), 0)
+                    sig_count[(hb, ch)] = cnt + 1
+                    nc.tensor.matmul_mx(
+                        out=sig[(hb, ch)][:],
+                        lhsT=hc[:, n, g, c0 : c0 + P].bitcast(FP8X4),
+                        lhsT_scale=hs[:, n, g, c0 : c0 + P],
+                        rhs=w2c[:, g, ch * 512 : (ch + 1) * 512].bitcast(FP8X4),
+                        rhs_scale=w2s[:, g, ch * 512 : (ch + 1) * 512],
+                        start=(cnt == 0),
+                        stop=(cnt == 4 * UNITS - 1),
+                    )
 
         def main_passes(n, ms):
             for m in ms:
@@ -213,106 +226,170 @@ def tile_nonlocalmp_pa_kernel(tc, F, W1, b1, W2, b2, out):
                         out=y[:],
                         lhsT=w2c[:, g, m * P : (m + 1) * P].bitcast(FP8X4),
                         lhsT_scale=w2s[:, g, m * P : (m + 1) * P],
-                        rhs=hct[n][:, g, :].bitcast(FP8X4),
-                        rhs_scale=hst[n][:, g, :],
+                        rhs=hc[:, n, g, :].bitcast(FP8X4),
+                        rhs_scale=hs[:, n, g, :],
                         start=(g == 0),
                         stop=(g == 1),
                     )
                 ytile[(n, m)] = y
 
-        def pe_block(n):
-            main_passes(n, range(0, 4))
-            sigma_passes(n, 0)
-            main_passes(n, range(4, 8))
-            sigma_passes(n, 1)
+        def pe_after_quant(n, g):
+            done_g[n] = done_g.get(n, 0) + 1
+            if done_g[n] == 1:
+                if state["w2"][g]:
+                    sigma_passes(n, g, 0)
+                    sigma_passes(n, g, 1)
+                else:
+                    state["sig_wait"] = state["sig_wait"] + [(n, g)]
+            else:
+                assert state["w2"][0] and state["w2"][1]
+                main_passes(n, range(0, 4))
+                sigma_passes(n, g, 0)
+                main_passes(n, range(4, 8))
+                sigma_passes(n, g, 1)
+                state["oq"] = state["oq"] + [(n, m) for m in range(8)]
 
         def flush():
-            k = state["pending"]
-            if k is None:
+            q = state["pending"]
+            if q is None:
                 return
             state["pending"] = None
-            n, g = k
+            n, g = SEQ[q][0], SEQ[q][1]
             nc.vector.quantize_mx(
-                out=hct[n][:, g, :].bitcast(FP8X4), scales=hst[n][:, g, :], in_=hbt[k][:]
+                out=hc[:, n, g, :].bitcast(FP8X4), scales=hs[:, n, g, :], in_=hbt[q][:]
             )
-            done_g[n] = done_g.get(n, 0) + 1
-            if done_g[n] == 2:
-                pe_block(n)
+            pe_after_quant(n, g)
 
-        def h_tile(n, g):
-            if n not in hct:
-                hct[n] = hcp.tile([P, 2, 512], U32, name="hc", align_bytes=64)
-                hst[n] = hcp.tile([P, 2, 512], U8, name="hs", align_bytes=64)
+        def emit_add(q):
+            n, g, eng = SEQ[q][0], SEQ[q][1], SEQ[q][2]
+            assert g == 0 or state["evac1"]
             u = up.tile([P, 2, SETS, NODES, 4], F32, name="u")
+            utile[q] = u
             a_view = a4[:, g].rearrange("p (b i) t -> p b i t", i=NODES)
             b_view = b4[:, g].rearrange("p (b j) t -> p b j t", j=NODES)
             for jj in range(2):
                 j = 2 * n + jj
-                nc.vector.tensor_tensor(
-                    out=u[:, jj],
-                    in0=a_view,
-                    in1=b_view[:, :, j, :].unsqueeze(2).to_broadcast([P, SETS, NODES, 4]),
-                    op=ALU.add,
-                )
-                flush()
-            hb16 = hbp.tile([P, 2048], BF16, name="hb16", align_bytes=64)
-            uf = u[:].rearrange("p a b i t -> p (a b i t)")
-            nc.vector.scalar_tensor_tensor(
-                out=hb16[:], in0=uf, scalar=SLOPE, in1=uf, op0=ALU.mult, op1=ALU.max
-            )
-            hbt[(n, g)] = hb16
-            state["pending"] = (n, g)
-
-        def o_part(n, half):
-            for m in range(4 * half, 4 * half + 4):
-                y = ytile[(n, m)]
-                if n == 0:
-                    nc.vector.tensor_scalar_max(out=acc[:, m, :], in0=y[:], scalar1=nb2[:, m : m + 1])
-                else:
-                    nc.vector.scalar_tensor_tensor(
-                        out=acc[:, m, :],
-                        in0=y[:],
-                        scalar=nb2[:, m : m + 1],
-                        in1=acc[:, m, :],
-                        op0=ALU.max,
-                        op1=ALU.add,
+                if eng == "V":
+                    nc.vector.tensor_tensor(
+                        out=u[:, jj],
+                        in0=a_view,
+                        in1=b_view[:, :, j, :].unsqueeze(2).to_broadcast([P, SETS, NODES, 4]),
+                        op=ALU.add,
                     )
-                flush()
+                    flush()
+                else:
+                    for bh in range(2):
+                        bs = slice(bh * 8, bh * 8 + 8)
+                        nc.gpsimd.tensor_tensor(
+                            out=u[:, jj, bs],
+                            in0=a_view[:, bs],
+                            in1=b_view[:, bs, j, :].unsqueeze(2).to_broadcast([P, 8, NODES, 4]),
+                            op=ALU.add,
+                        )
+
+        def emit_scalar_leaky(q):
+            uf = utile[q][:].rearrange("p a b i t -> p (a b i t)")
+            hb16 = hbp.tile([P, 2048], BF16, name="hb16", align_bytes=64)
+            nn = nnp.tile([P, 2048], BF16, name="nn")
+            nc.scalar.activation(out=hb16[:], in_=uf, func=ACT.Relu)
+            nc.scalar.activation(out=nn[:], in_=uf, func=ACT.Relu, scale=-SLOPE)
+            hbt[q] = hb16
+            nnt[q] = nn
+
+        def finish(q):
+            if SEQ[q][3] == "V":
+                uf = utile[q][:].rearrange("p a b i t -> p (a b i t)")
+                hb16 = hbp.tile([P, 2048], BF16, name="hb16", align_bytes=64)
+                nc.vector.scalar_tensor_tensor(
+                    out=hb16[:], in0=uf, scalar=SLOPE, in1=uf, op0=ALU.mult, op1=ALU.max
+                )
+                hbt[q] = hb16
+            else:
+                nc.vector.tensor_tensor(out=hbt[q][:], in0=hbt[q][:], in1=nnt[q][:], op=ALU.subtract)
+            flush()
+            state["pending"] = q
+
+        def o_one(n, m):
+            y = ytile[(n, m)]
+            if n == 0:
+                nc.vector.tensor_scalar_max(out=acc[:, m, :], in0=y[:], scalar1=nb2[:, m : m + 1])
+            else:
+                nc.vector.scalar_tensor_tensor(
+                    out=acc[:, m, :],
+                    in0=y[:],
+                    scalar=nb2[:, m : m + 1],
+                    in1=acc[:, m, :],
+                    op0=ALU.max,
+                    op1=ALU.add,
+                )
+            flush()
 
         def q1(idx):
             quant(g1[idx], w1c[:, 1, idx // 2, idx % 2, :], w1s[:, 1, idx // 2, idx % 2, :])
             flush()
+            if idx < 3:
+                g2[idx] = regroup(False, w2raw[(idx // 2, idx % 2)])
 
-        h_tile(0, 0)
-        q1(0)
-        q1(1)
-        h_tile(1, 0)
-        q1(2)
-        q1(3)
-        st = stage1_pe(1)
-        evac_b(1, st)
-        g2 = {}
-        for idx in range(4):
-            g2[idx] = regroup(False, w2raw[(idx // 2, idx % 2)])
-        h_tile(2, 0)
-        evac_a(1, st)
-        flush()
-        h_tile(0, 1)
-        for idx in range(4):
+        def qw2(idx):
             gg, ch = idx // 2, idx % 2
             quant(g2[idx], w2c[:, gg, ch * 512 : (ch + 1) * 512], w2s[:, gg, ch * 512 : (ch + 1) * 512])
-        h_tile(1, 1)
-        o_part(0, 0)
-        h_tile(2, 1)
-        o_part(0, 1)
-        for n in range(3, UNITS):
-            h_tile(n, 0)
-            o_part(n - 2, 0)
-            h_tile(n, 1)
-            o_part(n - 2, 1)
-        for n in range(UNITS - 2, UNITS):
-            o_part(n, 0)
-            o_part(n, 1)
+            flush()
+            if ch == 1:
+                state["w2"][gg] = True
+                for (n, g) in state["sig_wait"]:
+                    if g == gg:
+                        sigma_passes(n, g, 0)
+                        sigma_passes(n, g, 1)
+                state["sig_wait"] = [w for w in state["sig_wait"] if w[1] != gg]
+
+        def lookahead(q):
+            if SEQ[q][3] == "V":
+                return 0 if SEQ[q][2] == "V" else 2
+            return 2 if SEQ[q][2] == "V" else 3
+
+        added = set()
+        nslots = len(SEQ)
+        for s in range(nslots + 2):
+            for eng in ("G", "V"):
+                for q in range(nslots):
+                    if q not in added and SEQ[q][2] == eng and q - lookahead(q) <= s and lookahead(q) > 0:
+                        emit_add(q)
+                        added.add(q)
+            if s + 1 < nslots and SEQ[s + 1][3] == "S":
+                emit_scalar_leaky(s + 1)
+            if s == 2:
+                q1(3)
+                st = stage1_pe(1)
+                evac_b(1, st)
+                g2[3] = regroup(False, w2raw[(1, 1)])
+            if s < nslots:
+                if s not in added:
+                    emit_add(s)
+                    added.add(s)
+                finish(s)
+            if s == 0:
+                q1(0)
+            if s == 1:
+                q1(1)
+                q1(2)
+            if s == 2:
+                evac_a(1, st)
+                flush()
+                state["evac1"] = True
+            if s == 3:
+                qw2(0)
+                qw2(1)
+            if s == 4:
+                qw2(2)
+                qw2(3)
+            todo = state["oq"][: OCAP[s]]
+            state["oq"] = state["oq"][OCAP[s] :]
+            for (n, m) in todo:
+                o_one(n, m)
+        assert not state["oq"] and state["pending"] is None and not state["sig_wait"]
+
+        accs = up.tile([P, 8, ROWS], F32, name="u")
+        sigsb = up.tile([P, 4, 512], F32, name="u")
 
         for hb in range(2):
             for ch in range(2):

@@ -278,12 +278,12 @@ def tile_nonlocalmp_pa_kernel(tc, F, W1, b1, W2, b2, out):
                     )
                     flush()
                 else:
-                    for bh in range(2):
-                        bs = slice(bh * 8, bh * 8 + 8)
+                    for bh in range(4):
+                        bs = slice(bh * 4, bh * 4 + 4)
                         nc.gpsimd.tensor_tensor(
                             out=u[:, jj, bs],
                             in0=a_view[:, bs],
-                            in1=b_view[:, bs, j, :].unsqueeze(2).to_broadcast([P, 8, NODES, 4]),
+                            in1=b_view[:, bs, j, :].unsqueeze(2).to_broadcast([P, 4, NODES, 4]),
                             op=ALU.add,
                         )
 

@@ -26,8 +26,8 @@ FLOPS = 2 * ROWS * C * 2 * C + 2 * ROWS * NODES * C * C
 SEQ = [
     (0, 0, "V", "V"), (1, 0, "V", "V"), (2, 0, "V", "V"), (3, 0, "V", "V"),
     (4, 0, "V", "S"), (0, 1, "V", "S"), (5, 0, "V", "S"), (1, 1, "V", "S"),
-    (6, 0, "V", "S"), (2, 1, "G", "S"), (7, 0, "V", "S"), (3, 1, "G", "S"),
-    (4, 1, "V", "S"), (5, 1, "G", "S"), (6, 1, "G", "S"), (7, 1, "G", "S"),
+    (6, 0, "V", "S"), (2, 1, "V", "S"), (7, 0, "V", "S"), (3, 1, "V", "S"),
+    (4, 1, "V", "S"), (5, 1, "V", "S"), (6, 1, "V", "S"), (7, 1, "V", "S"),
 ]
 OCAP = [0, 0, 0, 0, 0, 0, 4, 4, 4, 4, 4, 4, 8, 8, 8, 8, 8, 8]
 
@@ -278,12 +278,12 @@ def tile_nonlocalmp_pa_kernel(tc, F, W1, b1, W2, b2, out):
                     )
                     flush()
                 else:
-                    for bh in range(4):
-                        bs = slice(bh * 4, bh * 4 + 4)
+                    for bh in range(2):
+                        bs = slice(bh * 8, bh * 8 + 8)
                         nc.gpsimd.tensor_tensor(
                             out=u[:, jj, bs],
                             in0=a_view[:, bs],
-                            in1=b_view[:, bs, j, :].unsqueeze(2).to_broadcast([P, 4, NODES, 4]),
+                            in1=b_view[:, bs, j, :].unsqueeze(2).to_broadcast([P, 8, NODES, 4]),
                             op=ALU.add,
                         )
 

@@ -23,13 +23,9 @@ SLOPE = 0.2
 FLOPS = 2 * ROWS * C * 2 * C + 2 * ROWS * NODES * C * C
 
 
-SEQ = [
-    (0, 0, "V", "V"), (1, 0, "V", "V"), (2, 0, "V", "V"), (3, 0, "V", "V"),
-    (4, 0, "V", "S"), (0, 1, "V", "S"), (5, 0, "V", "S"), (1, 1, "V", "S"),
-    (6, 0, "V", "S"), (2, 1, "V", "S"), (7, 0, "V", "S"), (3, 1, "V", "S"),
-    (4, 1, "V", "S"), (5, 1, "V", "S"), (6, 1, "V", "S"), (7, 1, "V", "S"),
-]
-OCAP = [0, 0, 0, 0, 0, 0, 4, 4, 4, 4, 4, 4, 8, 8, 8, 8, 8, 8]
+SEQ = [(n, g) for n in range(UNITS) for g in range(2)]
+VSHARE = 84
+V_COMBINE = [(7, m) for m in range(8)]
 
 
 def tile_nonlocalmp_pa_kernel(tc, F, W1, b1, W2, b2, out):
@@ -41,12 +37,12 @@ def tile_nonlocalmp_pa_kernel(tc, F, W1, b1, W2, b2, out):
         const = ctx.enter_context(tc.tile_pool(name="const", bufs=1))
         rawp = ctx.enter_context(tc.tile_pool(name="rawp", bufs=8))
         grpp = ctx.enter_context(tc.tile_pool(name="grpp", bufs=4))
-        up = ctx.enter_context(tc.tile_pool(name="up", bufs=5))
+        up = ctx.enter_context(tc.tile_pool(name="up", bufs=2))
         hbp = ctx.enter_context(tc.tile_pool(name="hbp", bufs=3))
-        nnp = ctx.enter_context(tc.tile_pool(name="nnp", bufs=2))
+        rlp = ctx.enter_context(tc.tile_pool(name="rlp", bufs=10))
         resp = ctx.enter_context(tc.tile_pool(name="resp", bufs=4))
         work = ctx.enter_context(tc.psum_pool(name="work", bufs=4))
-        sigp = ctx.enter_context(tc.psum_pool(name="sigp", bufs=1))
+        sump = ctx.enter_context(tc.psum_pool(name="sump", bufs=1))
         ctx.enter_context(tc.manual_schedule())
 
         ident32 = const.tile([P, P], F32, name="ident32")
@@ -69,15 +65,15 @@ def tile_nonlocalmp_pa_kernel(tc, F, W1, b1, W2, b2, out):
         a4 = const.tile([P, 2, ROWS, 4], F32, name="a4")
         b4 = const.tile([P, 2, ROWS, 4], F32, name="b4")
         b1c = const.tile([P, 8], F32, name="b1c")
-        nb2 = const.tile([P, 8], F32, name="nb2")
-        b2x = const.tile([P, 8], F32, name="b2x")
-        acc = const.tile([P, 8, 512], F32, name="acc")
+        b2r = const.tile([P, 8], F32, name="b2r")
+        b2row = const.tile([P, C], BF16, name="b2row")
 
+        nc.sync.dma_start(out=bt[0:8, :], in_=b1.rearrange("(r c) -> r c", c=P))
+        nc.sync.dma_start(out=bt[8:16, :], in_=b2.rearrange("(r c) -> r c", c=P))
         nc.sync.dma_start(out=fsb[:], in_=f_flat.rearrange("(f p) c -> p f c", p=P))
         w1raw = {}
         w2raw = {}
-
-        def load_w1(g):
+        for g in range(2):
             for ab in range(2):
                 for kp in range(2):
                     raw = rawp.tile([P, 4, 512], BF16, name="raw")
@@ -87,34 +83,35 @@ def tile_nonlocalmp_pa_kernel(tc, F, W1, b1, W2, b2, out):
                         in_=W1[r0 : r0 + 512, g * 512 : (g + 1) * 512].rearrange("(p j) w -> p j w", j=4),
                     )
                     w1raw[(g, ab, kp)] = raw
-
-        load_w1(0)
-        nc.sync.dma_start(out=bt[0:8, :], in_=b1.rearrange("(r c) -> r c", c=P))
-        nc.sync.dma_start(out=bt[8:16, :], in_=b2.rearrange("(r c) -> r c", c=P))
-        load_w1(1)
-        for g in range(2):
-            for ch in range(2):
+        for ch in range(2):
+            for g in range(2):
                 raw = rawp.tile([P, 4, 512], BF16, name="raw")
                 nc.sync.dma_start(
                     out=raw[:],
                     in_=W2[g * 512 : (g + 1) * 512, ch * 512 : (ch + 1) * 512].rearrange("(t p) n -> p t n", p=P),
                 )
                 w2raw[(g, ch)] = raw
+        nc.sync.dma_start(out=b2row[:], in_=b2.partition_broadcast(P))
 
-        def regroup(eng_is_vector, raw):
+        def regroup(raw, vshare):
             gq = grpp.tile([P, 512, 4], BF16, name="gq", align_bytes=64)
             dst = gq[:].rearrange("p (c i) t -> p c t i", i=4)
             src = raw[:].rearrange("p t (c i) -> p c t i", i=4)
-            if eng_is_vector:
-                nc.vector.tensor_copy(out=dst, in_=src)
-            else:
-                nc.scalar.copy(out=dst, in_=src)
+            if vshare > 0:
+                nc.vector.tensor_copy(out=dst[:, 0:vshare], in_=src[:, 0:vshare])
+            if vshare < 128:
+                nc.scalar.copy(out=dst[:, vshare:128], in_=src[:, vshare:128])
             return gq
 
         def quant(gq, codes, scales):
             nc.vector.quantize_mx(
                 out=codes.bitcast(FP8X4), scales=scales, in_=gq[:].rearrange("p w t -> p (w t)")
             )
+
+        btp = work.tile([P, P], BF16, name="wk")
+        nc.tensor.transpose(btp[:], bt[:], identb[:])
+        nc.vector.tensor_copy(out=b1c[:], in_=btp[:, 0:8])
+        nc.vector.tensor_scalar_mul(out=b2r[:], in0=btp[:, 8:16], scalar1=1.0 - SLOPE)
 
         fsb32 = fsb[:].bitcast(F32)
         fg32 = fg[:].bitcast(F32)
@@ -127,16 +124,15 @@ def tile_nonlocalmp_pa_kernel(tc, F, W1, b1, W2, b2, out):
                         fsb32[:, f, kp * 256 + u : (kp + 1) * 256 : 2],
                         ident32[:],
                     )
-            nc.vector.tensor_copy(out=fg32[:, kp], in_=xt[:].rearrange("p u c -> p c u"))
+            nc.scalar.copy(out=fg32[:, kp], in_=xt[:].rearrange("p u c -> p c u"))
         nc.vector.quantize_mx(
             out=fc[:].rearrange("p k c -> p (k c)").bitcast(FP8X4),
             scales=fs[:].rearrange("p k c -> p (k c)"),
             in_=fg[:].rearrange("p k c t -> p (k c t)"),
         )
 
-        def stage1_pe(g):
-            tiles = {}
-            for ab in range(2):
+        def stage1_pe(g, ab, tiles):
+            if True:
                 for f in range(2):
                     ps = work.tile([P, 4, P], F32, name="wk")
                     for t in range(4):
@@ -151,7 +147,6 @@ def tile_nonlocalmp_pa_kernel(tc, F, W1, b1, W2, b2, out):
                                 stop=(kp == 1),
                             )
                     tiles[(ab, f)] = ps
-            return tiles
 
         def evac_a(g, tiles):
             for f in range(2):
@@ -162,64 +157,41 @@ def tile_nonlocalmp_pa_kernel(tc, F, W1, b1, W2, b2, out):
                     op=ALU.add,
                 )
 
-        def evac_b(g, tiles):
-            for f in range(2):
-                nc.scalar.copy(
-                    out=b4[:, g, f * P : (f + 1) * P, :],
-                    in_=tiles[(1, f)][:].rearrange("p t r -> p r t"),
-                )
+        def evac_b(g, tiles, second_on_vector):
+            nc.scalar.copy(out=b4[:, g, 0:P, :], in_=tiles[(1, 0)][:].rearrange("p t r -> p r t"))
+            if second_on_vector:
+                nc.vector.tensor_copy(out=b4[:, g, P:ROWS, :], in_=tiles[(1, 1)][:].rearrange("p t r -> p r t"))
+            else:
+                nc.scalar.copy(out=b4[:, g, P:ROWS, :], in_=tiles[(1, 1)][:].rearrange("p t r -> p r t"))
 
+        def w1q(g, idx, gq):
+            quant(gq, w1c[:, g, idx // 2, idx % 2, :], w1s[:, g, idx // 2, idx % 2, :])
+
+        st0 = {}
         prev = None
         for idx in range(4):
-            gq = regroup(True, w1raw[(0, idx // 2, idx % 2)])
+            gq = regroup(w1raw[(0, idx // 2, idx % 2)], VSHARE)
             if prev is not None:
-                quant(prev[0], w1c[:, 0, prev[1] // 2, prev[1] % 2, :], w1s[:, 0, prev[1] // 2, prev[1] % 2, :])
+                w1q(0, prev[1], prev[0])
+                if prev[1] == 1:
+                    stage1_pe(0, 0, st0)
             prev = (gq, idx)
-        btp = work.tile([P, P], BF16, name="wk")
-        nc.tensor.transpose(btp[:], bt[:], identb[:])
-        nc.vector.tensor_copy(out=b1c[:], in_=btp[:, 0:8])
-        quant(prev[0], w1c[:, 0, 1, 1, :], w1s[:, 0, 1, 1, :])
-        nc.vector.tensor_scalar_mul(out=nb2[:], in0=btp[:, 8:16], scalar1=-1.0)
-        nc.vector.tensor_scalar_mul(out=b2x[:], in0=btp[:, 8:16], scalar1=float(NODES) / (1.0 - SLOPE))
-        st = stage1_pe(0)
-        evac_a(0, st)
-        evac_b(0, st)
+        w1q(0, 3, prev[0])
+        stage1_pe(0, 1, st0)
 
-        g1 = {}
-        for idx in range(4):
-            g1[idx] = regroup(False, w1raw[(1, idx // 2, idx % 2)])
-        g2 = {}
-
-        sig = {}
+        total = {}
         for hb in range(2):
             for ch in range(2):
-                sig[(hb, ch)] = sigp.tile([P, 512], F32, name="sig%d%d" % (hb, ch))
-        state = {"pending": None, "w2": [False, False], "evac1": False, "sig_wait": [], "oq": []}
-        sig_count = {}
+                total[(hb, ch)] = sump.tile([P, 512], F32, name="tot%d%d" % (hb, ch))
+        state = {"pending": None, "evac1": False, "w2": 0, "last_e": None}
+        tcount = {}
         utile = {}
         hbt = {}
-        nnt = {}
-        ytile = {}
+        rlt = {}
         done_g = {}
 
-        def sigma_passes(n, g, hb):
-            for ch in range(2):
-                for jj in range(2):
-                    c0 = jj * 256 + hb * P
-                    cnt = sig_count.get((hb, ch), 0)
-                    sig_count[(hb, ch)] = cnt + 1
-                    nc.tensor.matmul_mx(
-                        out=sig[(hb, ch)][:],
-                        lhsT=hc[:, n, g, c0 : c0 + P].bitcast(FP8X4),
-                        lhsT_scale=hs[:, n, g, c0 : c0 + P],
-                        rhs=w2c[:, g, ch * 512 : (ch + 1) * 512].bitcast(FP8X4),
-                        rhs_scale=w2s[:, g, ch * 512 : (ch + 1) * 512],
-                        start=(cnt == 0),
-                        stop=(cnt == 4 * UNITS - 1),
-                    )
-
-        def main_passes(n, ms):
-            for m in ms:
+        def main_and_leaky(n, half):
+            for m in range(4 * half, 4 * half + 4):
                 y = work.tile([P, 512], F32, name="wk")
                 for g in range(2):
                     nc.tensor.matmul_mx(
@@ -231,37 +203,59 @@ def tile_nonlocalmp_pa_kernel(tc, F, W1, b1, W2, b2, out):
                         start=(g == 0),
                         stop=(g == 1),
                     )
-                ytile[(n, m)] = y
-
-        def pe_after_quant(n, g):
-            done_g[n] = done_g.get(n, 0) + 1
-            if done_g[n] == 1:
-                if state["w2"][g]:
-                    sigma_passes(n, g, 0)
-                    sigma_passes(n, g, 1)
+                rl = rlp.tile([P, 2, 512], F32, name="rl")
+                nc.scalar.activation(
+                    out=rl[:, 0, :], in_=y[:], func=ACT.Relu, bias=b2r[:, m : m + 1], scale=1.0 - SLOPE
+                )
+                if (n, m) in V_COMBINE:
+                    nc.vector.scalar_tensor_tensor(
+                        out=rl[:, 1, :], in0=y[:], scalar=SLOPE, in1=rl[:, 0, :], op0=ALU.mult, op1=ALU.add
+                    )
                 else:
-                    state["sig_wait"] = state["sig_wait"] + [(n, g)]
-            else:
-                assert state["w2"][0] and state["w2"][1]
-                main_passes(n, range(0, 4))
-                sigma_passes(n, g, 0)
-                main_passes(n, range(4, 8))
-                sigma_passes(n, g, 1)
-                state["oq"] = state["oq"] + [(n, m) for m in range(8)]
+                    nc.scalar.mul(out=rl[:, 1, :], in_=y[:], mul=SLOPE)
+                rlt[(n, m)] = rl
+
+        def sum_transposes(n, half):
+            for m in range(4 * half, 4 * half + 4):
+                ch, mm = m // 4, m % 4
+                for term in ([1] if (n, m) in V_COMBINE else [0, 1]):
+                    for jj in range(2):
+                        for hb in range(2):
+                            c0 = jj * ROWS + hb * P
+                            cnt = tcount.get((hb, ch), 0)
+                            tcount[(hb, ch)] = cnt + 1
+                            nc.tensor.matmul(
+                                out=total[(hb, ch)][:, mm * P : (mm + 1) * P],
+                                lhsT=rlt[(n, m)][:, term, c0 : c0 + P],
+                                rhs=ident32[:],
+                                is_transpose=True,
+                                start=(cnt == 0),
+                                stop=(cnt == 16 * UNITS - 1 - len(V_COMBINE)),
+                            )
+
+        def stage2(n):
+            for half in range(2):
+                main_and_leaky(n, half)
+                if state["last_e"] is not None:
+                    sum_transposes(state["last_e"][0], state["last_e"][1])
+                state["last_e"] = (n, half)
 
         def flush():
             q = state["pending"]
             if q is None:
                 return
             state["pending"] = None
-            n, g = SEQ[q][0], SEQ[q][1]
+            n, g = SEQ[q]
             nc.vector.quantize_mx(
                 out=hc[:, n, g, :].bitcast(FP8X4), scales=hs[:, n, g, :], in_=hbt[q][:]
             )
-            pe_after_quant(n, g)
+            done_g[n] = done_g.get(n, 0) + 1
+            if done_g[n] == 2:
+                assert state["w2"] == 4
+                stage2(n)
 
-        def emit_add(q):
-            n, g, eng = SEQ[q][0], SEQ[q][1], SEQ[q][2]
+        def h_add(q):
+            n, g = SEQ[q]
             assert g == 0 or state["evac1"]
             u = up.tile([P, 2, SETS, NODES, 4], F32, name="u")
             utile[q] = u
@@ -269,153 +263,74 @@ def tile_nonlocalmp_pa_kernel(tc, F, W1, b1, W2, b2, out):
             b_view = b4[:, g].rearrange("p (b j) t -> p b j t", j=NODES)
             for jj in range(2):
                 j = 2 * n + jj
-                if eng == "V":
-                    nc.vector.tensor_tensor(
-                        out=u[:, jj],
-                        in0=a_view,
-                        in1=b_view[:, :, j, :].unsqueeze(2).to_broadcast([P, SETS, NODES, 4]),
-                        op=ALU.add,
-                    )
-                    flush()
-                else:
-                    for bh in range(2):
-                        bs = slice(bh * 8, bh * 8 + 8)
-                        nc.gpsimd.tensor_tensor(
-                            out=u[:, jj, bs],
-                            in0=a_view[:, bs],
-                            in1=b_view[:, bs, j, :].unsqueeze(2).to_broadcast([P, 8, NODES, 4]),
-                            op=ALU.add,
-                        )
+                nc.vector.tensor_tensor(
+                    out=u[:, jj],
+                    in0=a_view,
+                    in1=b_view[:, :, j, :].unsqueeze(2).to_broadcast([P, SETS, NODES, 4]),
+                    op=ALU.add,
+                )
+                flush()
 
-        def emit_scalar_leaky(q):
+        def h_leaky(q):
             uf = utile[q][:].rearrange("p a b i t -> p (a b i t)")
             hb16 = hbp.tile([P, 2048], BF16, name="hb16", align_bytes=64)
-            nn = nnp.tile([P, 2048], BF16, name="nn")
-            nc.scalar.activation(out=hb16[:], in_=uf, func=ACT.Relu)
-            nc.scalar.activation(out=nn[:], in_=uf, func=ACT.Relu, scale=-SLOPE)
+            nc.vector.scalar_tensor_tensor(
+                out=hb16[:], in0=uf, scalar=SLOPE, in1=uf, op0=ALU.mult, op1=ALU.max
+            )
             hbt[q] = hb16
-            nnt[q] = nn
-
-        def finish(q):
-            if SEQ[q][3] == "V":
-                uf = utile[q][:].rearrange("p a b i t -> p (a b i t)")
-                hb16 = hbp.tile([P, 2048], BF16, name="hb16", align_bytes=64)
-                nc.vector.scalar_tensor_tensor(
-                    out=hb16[:], in0=uf, scalar=SLOPE, in1=uf, op0=ALU.mult, op1=ALU.max
-                )
-                hbt[q] = hb16
-            else:
-                nc.vector.tensor_tensor(out=hbt[q][:], in0=hbt[q][:], in1=nnt[q][:], op=ALU.subtract)
-            flush()
             state["pending"] = q
 
-        def o_one(n, m):
-            y = ytile[(n, m)]
-            if n == 0:
-                nc.vector.tensor_scalar_max(out=acc[:, m, :], in0=y[:], scalar1=nb2[:, m : m + 1])
-            else:
-                nc.vector.scalar_tensor_tensor(
-                    out=acc[:, m, :],
-                    in0=y[:],
-                    scalar=nb2[:, m : m + 1],
-                    in1=acc[:, m, :],
-                    op0=ALU.max,
-                    op1=ALU.add,
-                )
-            flush()
+        W2ORDER = [(0, 0), (1, 0), (0, 1), (1, 1)]
 
-        def q1(idx):
-            quant(g1[idx], w1c[:, 1, idx // 2, idx % 2, :], w1s[:, 1, idx // 2, idx % 2, :])
-            flush()
-            if idx < 3:
-                g2[idx] = regroup(False, w2raw[(idx // 2, idx % 2)])
+        def qw2(idx, gq):
+            gg, ch = W2ORDER[idx]
+            quant(gq, w2c[:, gg, ch * 512 : (ch + 1) * 512], w2s[:, gg, ch * 512 : (ch + 1) * 512])
+            state["w2"] = state["w2"] + 1
 
-        def qw2(idx):
-            gg, ch = idx // 2, idx % 2
-            quant(g2[idx], w2c[:, gg, ch * 512 : (ch + 1) * 512], w2s[:, gg, ch * 512 : (ch + 1) * 512])
-            flush()
-            if ch == 1:
-                state["w2"][gg] = True
-                for (n, g) in state["sig_wait"]:
-                    if g == gg:
-                        sigma_passes(n, g, 0)
-                        sigma_passes(n, g, 1)
-                state["sig_wait"] = [w for w in state["sig_wait"] if w[1] != gg]
+        st1 = {}
+        g10 = regroup(w1raw[(1, 0, 0)], 0)
+        evac_a(0, st0)
+        evac_b(0, st0, False)
+        g11 = regroup(w1raw[(1, 0, 1)], 128)
+        g12 = regroup(w1raw[(1, 1, 0)], 0)
+        w1q(1, 0, g10)
+        w1q(1, 1, g11)
+        stage1_pe(1, 0, st1)
+        h_add(0)
+        g13 = regroup(w1raw[(1, 1, 1)], 128)
+        w2a = regroup(w2raw[W2ORDER[0]], 0)
+        w2b = regroup(w2raw[W2ORDER[1]], 0)
+        w1q(1, 2, g12)
+        w1q(1, 3, g13)
+        stage1_pe(1, 1, st1)
+        h_leaky(0)
+        evac_b(1, st1, False)
+        evac_a(1, st1)
+        state["evac1"] = True
+        flush()
+        w2c_ = regroup(w2raw[W2ORDER[2]], 0)
+        w2d_ = regroup(w2raw[W2ORDER[3]], 0)
+        h_add(1)
+        qw2(0, w2a)
+        qw2(1, w2b)
+        qw2(2, w2c_)
+        h_leaky(1)
+        qw2(3, w2d_)
+        flush()
+        for q in range(2, len(SEQ)):
+            h_add(q)
+            h_leaky(q)
+        flush()
+        sum_transposes(state["last_e"][0], state["last_e"][1])
 
-        def lookahead(q):
-            if SEQ[q][3] == "V":
-                return 0 if SEQ[q][2] == "V" else 2
-            return 2 if SEQ[q][2] == "V" else 3
-
-        added = set()
-        nslots = len(SEQ)
-        for s in range(nslots + 2):
-            for eng in ("G", "V"):
-                for q in range(nslots):
-                    if q not in added and SEQ[q][2] == eng and q - lookahead(q) <= s and lookahead(q) > 0:
-                        emit_add(q)
-                        added.add(q)
-            if s + 1 < nslots and SEQ[s + 1][3] == "S":
-                emit_scalar_leaky(s + 1)
-            if s == 2:
-                q1(3)
-                st = stage1_pe(1)
-                evac_b(1, st)
-                g2[3] = regroup(False, w2raw[(1, 1)])
-            if s < nslots:
-                if s not in added:
-                    emit_add(s)
-                    added.add(s)
-                finish(s)
-            if s == 0:
-                q1(0)
-            if s == 1:
-                q1(1)
-                q1(2)
-            if s == 2:
-                evac_a(1, st)
-                flush()
-                state["evac1"] = True
-            if s == 3:
-                qw2(0)
-                qw2(1)
-            if s == 4:
-                qw2(2)
-                qw2(3)
-            todo = state["oq"][: OCAP[s]]
-            state["oq"] = state["oq"][OCAP[s] :]
-            for (n, m) in todo:
-                o_one(n, m)
-        assert not state["oq"] and state["pending"] is None and not state["sig_wait"]
-
-        accs = up.tile([P, 8, ROWS], F32, name="u")
-        sigsb = up.tile([P, 4, 512], F32, name="u")
-
-        for hb in range(2):
-            for ch in range(2):
-                nc.scalar.mul(out=sigsb[:, 2 * hb + ch, :], in_=sig[(hb, ch)][:], mul=SLOPE)
-        for m in range(8):
-            nc.vector.scalar_tensor_tensor(
-                out=accs[:, m, :],
-                in0=acc[:, m, 0:256],
-                scalar=b2x[:, m : m + 1],
-                in1=acc[:, m, 256:512],
-                op0=ALU.add,
-                op1=ALU.add,
-            )
         for ch in range(2):
             for hb in range(2):
-                tp = work.tile([P, 4, P], F32, name="wk")
-                for mm in range(4):
-                    nc.tensor.transpose(
-                        tp[:, mm, :], accs[:, 4 * ch + mm, hb * P : (hb + 1) * P], ident32[:]
-                    )
                 res = resp.tile([P, 512], F32, name="res")
                 nc.vector.scalar_tensor_tensor(
                     out=res[:],
-                    in0=tp[:].rearrange("p m r -> p (m r)"),
-                    scalar=1.0 - SLOPE,
-                    in1=sigsb[:, 2 * hb + ch, :],
+                    in0=b2row[:, ch * 512 : (ch + 1) * 512],
+                    scalar=SLOPE * NODES,
+                    in1=total[(hb, ch)][:],
                     op0=ALU.mult,
                     op1=ALU.add,
                 )

@@ -23,9 +23,10 @@ SLOPE = 0.2
 FLOPS = 2 * ROWS * C * 2 * C + 2 * ROWS * NODES * C * C
 
 
-SEQ = [(n, g) for n in range(UNITS) for g in range(2)]
+SEQ = [(n, g) for n in range(NODES) for g in range(2)]
 VSHARE = 84
-V_COMBINE = [(7, m) for m in range(8)]
+V_COMBINE = [13, 14, 15]
+LAG = 2
 
 
 def tile_nonlocalmp_pa_kernel(tc, F, W1, b1, W2, b2, out):
@@ -60,8 +61,8 @@ def tile_nonlocalmp_pa_kernel(tc, F, W1, b1, W2, b2, out):
         w1s = const.tile([P, 2, 2, 2, 512], U8, name="w1s", align_bytes=64)
         w2c = const.tile([P, 2, C], U32, name="w2c", align_bytes=64)
         w2s = const.tile([P, 2, C], U8, name="w2s", align_bytes=64)
-        hc = const.tile([P, UNITS, 2, 512], U32, name="hc", align_bytes=64)
-        hs = const.tile([P, UNITS, 2, 512], U8, name="hs", align_bytes=64)
+        hc = const.tile([P, NODES, 2, ROWS], U32, name="hc", align_bytes=64)
+        hs = const.tile([P, NODES, 2, ROWS], U8, name="hs", align_bytes=64)
         a4 = const.tile([P, 2, ROWS, 4], F32, name="a4")
         b4 = const.tile([P, 2, ROWS, 4], F32, name="b4")
         b1c = const.tile([P, 8], F32, name="b1c")
@@ -183,62 +184,72 @@ def tile_nonlocalmp_pa_kernel(tc, F, W1, b1, W2, b2, out):
         for hb in range(2):
             for ch in range(2):
                 total[(hb, ch)] = sump.tile([P, 512], F32, name="tot%d%d" % (hb, ch))
-        state = {"pending": None, "evac1": False, "w2": 0, "last_e": None}
+        state = {"pending": None, "evac1": False, "w2": 0, "last_e": None, "ready": []}
         tcount = {}
         utile = {}
         hbt = {}
         rlt = {}
+        ytile = {}
         done_g = {}
 
-        def main_and_leaky(n, half):
-            for m in range(4 * half, 4 * half + 4):
-                y = work.tile([P, 512], F32, name="wk")
-                for g in range(2):
-                    nc.tensor.matmul_mx(
-                        out=y[:],
-                        lhsT=w2c[:, g, m * P : (m + 1) * P].bitcast(FP8X4),
-                        lhsT_scale=w2s[:, g, m * P : (m + 1) * P],
-                        rhs=hc[:, n, g, :].bitcast(FP8X4),
-                        rhs_scale=hs[:, n, g, :],
-                        start=(g == 0),
-                        stop=(g == 1),
+        def main_and_leaky(n):
+            for k in range(4):
+                y = work.tile([P, 2, ROWS], F32, name="wk")
+                for mloc in range(2):
+                    m = 2 * k + mloc
+                    for g in range(2):
+                        nc.tensor.matmul_mx(
+                            out=y[:, mloc, :],
+                            lhsT=w2c[:, g, m * P : (m + 1) * P].bitcast(FP8X4),
+                            lhsT_scale=w2s[:, g, m * P : (m + 1) * P],
+                            rhs=hc[:, n, g, :].bitcast(FP8X4),
+                            rhs_scale=hs[:, n, g, :],
+                            start=(g == 0),
+                            stop=(g == 1),
+                        )
+                rl = rlp.tile([P, 2, 2, ROWS], F32, name="rl")
+                for mloc in range(2):
+                    m = 2 * k + mloc
+                    nc.scalar.activation(
+                        out=rl[:, 0, mloc, :], in_=y[:, mloc, :], func=ACT.Relu, bias=b2r[:, m : m + 1], scale=1.0 - SLOPE
                     )
-                rl = rlp.tile([P, 2, 512], F32, name="rl")
-                nc.scalar.activation(
-                    out=rl[:, 0, :], in_=y[:], func=ACT.Relu, bias=b2r[:, m : m + 1], scale=1.0 - SLOPE
-                )
-                if (n, m) in V_COMBINE:
-                    nc.vector.scalar_tensor_tensor(
-                        out=rl[:, 1, :], in0=y[:], scalar=SLOPE, in1=rl[:, 0, :], op0=ALU.mult, op1=ALU.add
-                    )
-                else:
-                    nc.scalar.mul(out=rl[:, 1, :], in_=y[:], mul=SLOPE)
-                rlt[(n, m)] = rl
+                if n not in V_COMBINE:
+                    nc.scalar.mul(out=rl[:, 1], in_=y[:], mul=SLOPE)
+                rlt[(n, k)] = rl
+                ytile[(n, k)] = y
 
-        def sum_transposes(n, half):
-            for m in range(4 * half, 4 * half + 4):
-                ch, mm = m // 4, m % 4
-                for term in ([1] if (n, m) in V_COMBINE else [0, 1]):
-                    for jj in range(2):
-                        for hb in range(2):
-                            c0 = jj * ROWS + hb * P
-                            cnt = tcount.get((hb, ch), 0)
-                            tcount[(hb, ch)] = cnt + 1
-                            nc.tensor.matmul(
-                                out=total[(hb, ch)][:, mm * P : (mm + 1) * P],
-                                lhsT=rlt[(n, m)][:, term, c0 : c0 + P],
-                                rhs=ident32[:],
-                                is_transpose=True,
-                                start=(cnt == 0),
-                                stop=(cnt == 16 * UNITS - 1 - len(V_COMBINE)),
-                            )
+        def combine(n):
+            if n in V_COMBINE:
+                for k in range(4):
+                    rl = rlt[(n, k)]
+                    nc.vector.scalar_tensor_tensor(
+                        out=rl[:, 1], in0=ytile[(n, k)][:], scalar=SLOPE, in1=rl[:, 0], op0=ALU.mult, op1=ALU.add
+                    )
+
+        def sum_transposes(n):
+            for hb in range(2):
+                for m in range(8):
+                    ch, mm = m // 4, m % 4
+                    for term in ([1] if n in V_COMBINE else [0, 1]):
+                        cnt = tcount.get((hb, ch), 0)
+                        tcount[(hb, ch)] = cnt + 1
+                        nc.tensor.matmul(
+                            out=total[(hb, ch)][:, mm * P : (mm + 1) * P],
+                            lhsT=rlt[(n, m // 2)][:, term, m % 2, hb * P : (hb + 1) * P],
+                            rhs=ident32[:],
+                            is_transpose=True,
+                            start=(cnt == 0),
+                            stop=(cnt == 4 * (2 * NODES - len(V_COMBINE)) - 1),
+                        )
 
         def stage2(n):
-            for half in range(2):
-                main_and_leaky(n, half)
-                if state["last_e"] is not None:
-                    sum_transposes(state["last_e"][0], state["last_e"][1])
-                state["last_e"] = (n, half)
+            assert state["w2"] == 4
+            if state["last_e"] is not None:
+                combine(state["last_e"])
+            main_and_leaky(n)
+            if state["last_e"] is not None:
+                sum_transposes(state["last_e"])
+            state["last_e"] = n
 
         def flush():
             q = state["pending"]
@@ -251,29 +262,31 @@ def tile_nonlocalmp_pa_kernel(tc, F, W1, b1, W2, b2, out):
             )
             done_g[n] = done_g.get(n, 0) + 1
             if done_g[n] == 2:
-                assert state["w2"] == 4
-                stage2(n)
+                state["ready"] = state["ready"] + [(n, q)]
+
+        def emit_ready(q_now):
+            while state["ready"] and state["ready"][0][1] + LAG <= q_now:
+                stage2(state["ready"][0][0])
+                state["ready"] = state["ready"][1:]
 
         def h_add(q):
             n, g = SEQ[q]
             assert g == 0 or state["evac1"]
-            u = up.tile([P, 2, SETS, NODES, 4], F32, name="u")
+            u = up.tile([P, SETS, NODES, 4], F32, name="u")
             utile[q] = u
             a_view = a4[:, g].rearrange("p (b i) t -> p b i t", i=NODES)
             b_view = b4[:, g].rearrange("p (b j) t -> p b j t", j=NODES)
-            for jj in range(2):
-                j = 2 * n + jj
-                nc.vector.tensor_tensor(
-                    out=u[:, jj],
-                    in0=a_view,
-                    in1=b_view[:, :, j, :].unsqueeze(2).to_broadcast([P, SETS, NODES, 4]),
-                    op=ALU.add,
-                )
-                flush()
+            nc.vector.tensor_tensor(
+                out=u[:],
+                in0=a_view,
+                in1=b_view[:, :, n, :].unsqueeze(2).to_broadcast([P, SETS, NODES, 4]),
+                op=ALU.add,
+            )
+            flush()
 
         def h_leaky(q):
-            uf = utile[q][:].rearrange("p a b i t -> p (a b i t)")
-            hb16 = hbp.tile([P, 2048], BF16, name="hb16", align_bytes=64)
+            uf = utile[q][:].rearrange("p b i t -> p (b i t)")
+            hb16 = hbp.tile([P, 4 * ROWS], BF16, name="hb16", align_bytes=64)
             nc.vector.scalar_tensor_tensor(
                 out=hb16[:], in0=uf, scalar=SLOPE, in1=uf, op0=ALU.mult, op1=ALU.max
             )
@@ -313,15 +326,18 @@ def tile_nonlocalmp_pa_kernel(tc, F, W1, b1, W2, b2, out):
         h_add(1)
         qw2(0, w2a)
         qw2(1, w2b)
-        qw2(2, w2c_)
         h_leaky(1)
-        qw2(3, w2d_)
+        qw2(2, w2c_)
         flush()
+        qw2(3, w2d_)
         for q in range(2, len(SEQ)):
             h_add(q)
+            emit_ready(q)
             h_leaky(q)
         flush()
-        sum_transposes(state["last_e"][0], state["last_e"][1])
+        emit_ready(len(SEQ) + LAG)
+        combine(state["last_e"])
+        sum_transposes(state["last_e"])
 
         for ch in range(2):
             for hb in range(2):

from contextlib import ExitStack

import concourse.bass as bass
import concourse.mybir as mybir
import concourse.tile as tile
from concourse.masks import make_identity

F32 = mybir.dt.float32
BF16 = mybir.dt.bfloat16
U32 = mybir.dt.uint32
U8 = mybir.dt.uint8
FP8X4 = mybir.dt.float8_e4m3fn_x4
ALU = mybir.AluOpType
ACT = mybir.ActivationFunctionType

P = 128
C = 1024
ROWS = 256
NODES = 16
SETS = 16
UNITS = 8
SLOPE = 0.2
FLOPS = 2 * ROWS * C * 2 * C + 2 * ROWS * NODES * C * C


SEQ = [(n, g) for n in range(NODES) for g in range(2)]
VSHARE = 84
V_COMBINE = [13, 14, 15]
LAG = 2


def tile_nonlocalmp_pa_kernel(tc, F, W1, b1, W2, b2, out):
    nc = tc.nc
    f_flat = F.flatten_outer_dims()
    out_flat = out.flatten_outer_dims()

    with ExitStack() as ctx:
        const = ctx.enter_context(tc.tile_pool(name="const", bufs=1))
        rawp = ctx.enter_context(tc.tile_pool(name="rawp", bufs=8))
        grpp = ctx.enter_context(tc.tile_pool(name="grpp", bufs=4))
        up = ctx.enter_context(tc.tile_pool(name="up", bufs=2))
        hbp = ctx.enter_context(tc.tile_pool(name="hbp", bufs=3))
        rlp = ctx.enter_context(tc.tile_pool(name="rlp", bufs=10))
        resp = ctx.enter_context(tc.tile_pool(name="resp", bufs=4))
        work = ctx.enter_context(tc.psum_pool(name="work", bufs=4))
        sump = ctx.enter_context(tc.psum_pool(name="sump", bufs=1))
        ctx.enter_context(tc.manual_schedule())

        ident32 = const.tile([P, P], F32, name="ident32")
        make_identity(nc, ident32[:])
        identb = const.tile([P, P], BF16, name="identb")
        make_identity(nc, identb[:])
        bt = const.tile([P, P], BF16, name="bt")
        nc.vector.memset(bt[:], 0.0)

        fsb = const.tile([P, 2, C], BF16, name="fsb")
        fg = const.tile([P, 2, ROWS, 4], BF16, name="fg", align_bytes=64)
        fc = const.tile([P, 2, ROWS], U32, name="fc", align_bytes=64)
        fs = const.tile([P, 2, ROWS], U8, name="fs", align_bytes=64)
        w1c = const.tile([P, 2, 2, 2, 512], U32, name="w1c", align_bytes=64)
        w1s = const.tile([P, 2, 2, 2, 512], U8, name="w1s", align_bytes=64)
        w2c = const.tile([P, 2, C], U32, name="w2c", align_bytes=64)
        w2s = const.tile([P, 2, C], U8, name="w2s", align_bytes=64)
        hc = const.tile([P, NODES, 2, ROWS], U32, name="hc", align_bytes=64)
        hs = const.tile([P, NODES, 2, ROWS], U8, name="hs", align_bytes=64)
        a4 = const.tile([P, 2, ROWS, 4], F32, name="a4")
        b4 = const.tile([P, 2, ROWS, 4], F32, name="b4")
        b1c = const.tile([P, 8], F32, name="b1c")
        b2r = const.tile([P, 8], F32, name="b2r")
        b2row = const.tile([P, C], BF16, name="b2row")

        nc.sync.dma_start(out=bt[0:8, :], in_=b1.rearrange("(r c) -> r c", c=P))
        nc.sync.dma_start(out=bt[8:16, :], in_=b2.rearrange("(r c) -> r c", c=P))
        nc.sync.dma_start(out=fsb[:], in_=f_flat.rearrange("(f p) c -> p f c", p=P))
        w1raw = {}
        w2raw = {}
        for g in range(2):
            for ab in range(2):
                for kp in range(2):
                    raw = rawp.tile([P, 4, 512], BF16, name="raw")
                    r0 = ab * C + kp * 512
                    nc.sync.dma_start(
                        out=raw[:],
                        in_=W1[r0 : r0 + 512, g * 512 : (g + 1) * 512].rearrange("(p j) w -> p j w", j=4),
                    )
                    w1raw[(g, ab, kp)] = raw
        for ch in range(2):
            for g in range(2):
                raw = rawp.tile([P, 4, 512], BF16, name="raw")
                nc.sync.dma_start(
                    out=raw[:],
                    in_=W2[g * 512 : (g + 1) * 512, ch * 512 : (ch + 1) * 512].rearrange("(t p) n -> p t n", p=P),
                )
                w2raw[(g, ch)] = raw
        nc.sync.dma_start(out=b2row[:], in_=b2.partition_broadcast(P))

        def regroup(raw, vshare):
            gq = grpp.tile([P, 512, 4], BF16, name="gq", align_bytes=64)
            dst = gq[:].rearrange("p (c i) t -> p c t i", i=4)
            src = raw[:].rearrange("p t (c i) -> p c t i", i=4)
            if vshare > 0:
                nc.vector.tensor_copy(out=dst[:, 0:vshare], in_=src[:, 0:vshare])
            if vshare < 128:
                nc.scalar.copy(out=dst[:, vshare:128], in_=src[:, vshare:128])
            return gq

        def quant(gq, codes, scales):
            nc.vector.quantize_mx(
                out=codes.bitcast(FP8X4), scales=scales, in_=gq[:].rearrange("p w t -> p (w t)")
            )

        btp = work.tile([P, P], BF16, name="wk")
        nc.tensor.transpose(btp[:], bt[:], identb[:])
        nc.vector.tensor_copy(out=b1c[:], in_=btp[:, 0:8])
        nc.vector.tensor_scalar_mul(out=b2r[:], in0=btp[:, 8:16], scalar1=1.0 - SLOPE)

        fsb32 = fsb[:].bitcast(F32)
        fg32 = fg[:].bitcast(F32)
        for kp in range(2):
            xt = work.tile([P, 2, ROWS], F32, name="wk")
            for f in range(2):
                for u in range(2):
                    nc.tensor.transpose(
                        xt[:, u, f * P : (f + 1) * P],
                        fsb32[:, f, kp * 256 + u : (kp + 1) * 256 : 2],
                        ident32[:],
                    )
            nc.scalar.copy(out=fg32[:, kp], in_=xt[:].rearrange("p u c -> p c u"))
        nc.vector.quantize_mx(
            out=fc[:].rearrange("p k c -> p (k c)").bitcast(FP8X4),
            scales=fs[:].rearrange("p k c -> p (k c)"),
            in_=fg[:].rearrange("p k c t -> p (k c t)"),
        )

        def stage1_pe(g, ab, tiles):
            if True:
                for f in range(2):
                    ps = work.tile([P, 4, P], F32, name="wk")
                    for t in range(4):
                        for kp in range(2):
                            nc.tensor.matmul_mx(
                                out=ps[:, t, :],
                                lhsT=w1c[:, g, ab, kp, t * P : (t + 1) * P].bitcast(FP8X4),
                                lhsT_scale=w1s[:, g, ab, kp, t * P : (t + 1) * P],
                                rhs=fc[:, kp, f * P : (f + 1) * P].bitcast(FP8X4),
                                rhs_scale=fs[:, kp, f * P : (f + 1) * P],
                                start=(kp == 0),
                                stop=(kp == 1),
                            )
                    tiles[(ab, f)] = ps

        def evac_a(g, tiles):
            for f in range(2):
                nc.vector.tensor_tensor(
                    out=a4[:, g, f * P : (f + 1) * P, :],
                    in0=tiles[(0, f)][:].rearrange("p t r -> p r t"),
                    in1=b1c[:, 4 * g : 4 * g + 4].unsqueeze(1).to_broadcast([P, P, 4]),
                    op=ALU.add,
                )

        def evac_b(g, tiles, second_on_vector):
            nc.scalar.copy(out=b4[:, g, 0:P, :], in_=tiles[(1, 0)][:].rearrange("p t r -> p r t"))
            if second_on_vector:
                nc.vector.tensor_copy(out=b4[:, g, P:ROWS, :], in_=tiles[(1, 1)][:].rearrange("p t r -> p r t"))
            else:
                nc.scalar.copy(out=b4[:, g, P:ROWS, :], in_=tiles[(1, 1)][:].rearrange("p t r -> p r t"))

        def w1q(g, idx, gq):
            quant(gq, w1c[:, g, idx // 2, idx % 2, :], w1s[:, g, idx // 2, idx % 2, :])

        st0 = {}
        prev = None
        for idx in range(4):
            gq = regroup(w1raw[(0, idx // 2, idx % 2)], VSHARE)
            if prev is not None:
                w1q(0, prev[1], prev[0])
                if prev[1] == 1:
                    stage1_pe(0, 0, st0)
            prev = (gq, idx)
        w1q(0, 3, prev[0])
        stage1_pe(0, 1, st0)

        total = {}
        for hb in range(2):
            for ch in range(2):
                total[(hb, ch)] = sump.tile([P, 512], F32, name="tot%d%d" % (hb, ch))
        state = {"pending": None, "evac1": False, "w2": 0, "last_e": None, "ready": []}
        tcount = {}
        utile = {}
        hbt = {}
        rlt = {}
        ytile = {}
        done_g = {}

        def main_and_leaky(n):
            for k in range(4):
                y = work.tile([P, 2, ROWS], F32, name="wk")
                for mloc in range(2):
                    m = 2 * k + mloc
                    for g in range(2):
                        nc.tensor.matmul_mx(
                            out=y[:, mloc, :],
                            lhsT=w2c[:, g, m * P : (m + 1) * P].bitcast(FP8X4),
                            lhsT_scale=w2s[:, g, m * P : (m + 1) * P],
                            rhs=hc[:, n, g, :].bitcast(FP8X4),
                            rhs_scale=hs[:, n, g, :],
                            start=(g == 0),
                            stop=(g == 1),
                        )
                rl = rlp.tile([P, 2, 2, ROWS], F32, name="rl")
                for mloc in range(2):
                    m = 2 * k + mloc
                    nc.scalar.activation(
                        out=rl[:, 0, mloc, :], in_=y[:, mloc, :], func=ACT.Relu, bias=b2r[:, m : m + 1], scale=1.0 - SLOPE
                    )
                if n not in V_COMBINE:
                    nc.scalar.mul(out=rl[:, 1], in_=y[:], mul=SLOPE)
                rlt[(n, k)] = rl
                ytile[(n, k)] = y

        def combine(n):
            if n in V_COMBINE:
                for k in range(4):
                    rl = rlt[(n, k)]
                    nc.vector.scalar_tensor_tensor(
                        out=rl[:, 1], in0=ytile[(n, k)][:], scalar=SLOPE, in1=rl[:, 0], op0=ALU.mult, op1=ALU.add
                    )

        def sum_transposes(n):
            for hb in range(2):
                for m in range(8):
                    ch, mm = m // 4, m % 4
                    for term in ([1] if n in V_COMBINE else [0, 1]):
                        cnt = tcount.get((hb, ch), 0)
                        tcount[(hb, ch)] = cnt + 1
                        nc.tensor.matmul(
                            out=total[(hb, ch)][:, mm * P : (mm + 1) * P],
                            lhsT=rlt[(n, m // 2)][:, term, m % 2, hb * P : (hb + 1) * P],
                            rhs=ident32[:],
                            is_transpose=True,
                            start=(cnt == 0),
                            stop=(cnt == 4 * (2 * NODES - len(V_COMBINE)) - 1),
                        )

        def stage2(n):
            assert state["w2"] == 4
            if state["last_e"] is not None:
                combine(state["last_e"])
            main_and_leaky(n)
            if state["last_e"] is not None:
                sum_transposes(state["last_e"])
            state["last_e"] = n

        def flush():
            q = state["pending"]
            if q is None:
                return
            state["pending"] = None
            n, g = SEQ[q]
            nc.vector.quantize_mx(
                out=hc[:, n, g, :].bitcast(FP8X4), scales=hs[:, n, g, :], in_=hbt[q][:]
            )
            done_g[n] = done_g.get(n, 0) + 1
            if done_g[n] == 2:
                state["ready"] = state["ready"] + [(n, q)]

        def emit_ready(q_now):
            while state["ready"] and state["ready"][0][1] + LAG <= q_now:
                stage2(state["ready"][0][0])
                state["ready"] = state["ready"][1:]

        def h_add(q):
            n, g = SEQ[q]
            assert g == 0 or state["evac1"]
            u = up.tile([P, SETS, NODES, 4], F32, name="u")
            utile[q] = u
            a_view = a4[:, g].rearrange("p (b i) t -> p b i t", i=NODES)
            b_view = b4[:, g].rearrange("p (b j) t -> p b j t", j=NODES)
            nc.vector.tensor_tensor(
                out=u[:],
                in0=a_view,
                in1=b_view[:, :, n, :].unsqueeze(2).to_broadcast([P, SETS, NODES, 4]),
                op=ALU.add,
            )
            flush()

        def h_leaky(q):
            uf = utile[q][:].rearrange("p b i t -> p (b i t)")
            hb16 = hbp.tile([P, 4 * ROWS], BF16, name="hb16", align_bytes=64)
            nc.vector.scalar_tensor_tensor(
                out=hb16[:], in0=uf, scalar=SLOPE, in1=uf, op0=ALU.mult, op1=ALU.max
            )
            hbt[q] = hb16
            state["pending"] = q

        W2ORDER = [(0, 0), (1, 0), (0, 1), (1, 1)]

        def qw2(idx, gq):
            gg, ch = W2ORDER[idx]
            quant(gq, w2c[:, gg, ch * 512 : (ch + 1) * 512], w2s[:, gg, ch * 512 : (ch + 1) * 512])
            state["w2"] = state["w2"] + 1

        st1 = {}
        g10 = regroup(w1raw[(1, 0, 0)], 0)
        evac_a(0, st0)
        evac_b(0, st0, False)
        g11 = regroup(w1raw[(1, 0, 1)], 128)
        g12 = regroup(w1raw[(1, 1, 0)], 0)
        w1q(1, 0, g10)
        w1q(1, 1, g11)
        stage1_pe(1, 0, st1)
        h_add(0)
        g13 = regroup(w1raw[(1, 1, 1)], 128)
        w2a = regroup(w2raw[W2ORDER[0]], 0)
        w2b = regroup(w2raw[W2ORDER[1]], 0)
        w1q(1, 2, g12)
        w1q(1, 3, g13)
        stage1_pe(1, 1, st1)
        h_leaky(0)
        evac_b(1, st1, False)
        evac_a(1, st1)
        state["evac1"] = True
        flush()
        w2c_ = regroup(w2raw[W2ORDER[2]], 0)
        w2d_ = regroup(w2raw[W2ORDER[3]], 0)
        h_add(1)
        qw2(0, w2a)
        qw2(1, w2b)
        h_leaky(1)
        qw2(2, w2c_)
        flush()
        qw2(3, w2d_)
        for q in range(2, len(SEQ)):
            h_add(q)
            emit_ready(q)
            h_leaky(q)
        flush()
        emit_ready(len(SEQ) + LAG)
        combine(state["last_e"])
        sum_transposes(state["last_e"])

        for ch in range(2):
            for hb in range(2):
                res = resp.tile([P, 512], F32, name="res")
                nc.vector.scalar_tensor_tensor(
                    out=res[:],
                    in0=b2row[:, ch * 512 : (ch + 1) * 512],
                    scalar=SLOPE * NODES,
                    in1=total[(hb, ch)][:],
                    op0=ALU.mult,
                    op1=ALU.add,
                )
                nc.sync.dma_start(
                    out=out_flat[hb * P : (hb + 1) * P, ch * 512 : (ch + 1) * 512], in_=res[:]
                )
